import numpy as np
import ml_dtypes

BF16 = ml_dtypes.bfloat16


def bf(x):
    return np.asarray(x, np.float32).astype(BF16)


def f32(x):
    return np.asarray(x, np.float32)


def f64(x):
    return np.asarray(x).astype(np.float64)


def striped(idx):
    return np.tile(idx.reshape(-1, 16).T, (8, 1))


V, D, M, L, B, T, K, N = 256, 128, 256, 128, 128, 8, 4, 1024


def setup_inputs():
    return {
        "table": bf(np.random.standard_normal((D, V))),
        "w1": bf(np.random.standard_normal((D, M)) / np.sqrt(D)),
        "scores": f32(0.5 + np.random.uniform(0.0, 1.0, (1, N))),
        "b1": f32(0.1 * np.random.standard_normal((M, 1))),
        "wout": bf(2.0 * np.random.standard_normal((M, L)) / np.sqrt(M)),
        "bout": f32(0.2 * np.random.standard_normal((L, 1))),
        "offs": striped(np.concatenate([np.random.permutation(V) for _ in range(K)])),
    }


def reference(table, w1, scores, b1, wout, bout, offs):
    idx = offs[:16].T.reshape(-1)
    h = (f64(w1).T @ f64(table)[:, idx]) * f64(scores)
    x = h.reshape(M, B, T).mean(axis=2) + f64(b1)
    z = x.T @ f64(wout) + f64(bout).T
    top = z.max(axis=1, keepdims=True)
    return z - top - np.log(np.exp(z - top).sum(axis=1, keepdims=True))

@@ -1,0 +1,102 @@
+import concourse.mybir as mybir
+
+BF16, F32, U16 = mybir.dt.bfloat16, mybir.dt.float32, mybir.dt.uint16
+ALU = mybir.AluOpType
+ACT = mybir.ActivationFunctionType
+
+P = 128
+WORDS = 256
+HIDDEN_BLOCKS = 2
+LABELS = 128
+SENTENCES = 128
+PER_SENTENCE = 8
+ENTRIES = SENTENCES * PER_SENTENCE
+PIECE = 256
+BANK = 512
+
+FLOPS = 2 * P * HIDDEN_BLOCKS * P * ENTRIES + 2 * HIDDEN_BLOCKS * P * SENTENCES * LABELS
+
+
+def tile_dnn_kernel(tc, table, w1, scores, b1, wout, bout, offs, out):
+    nc = tc.nc
+    with (
+        tc.tile_pool(name="held", bufs=1) as held,
+        tc.tile_pool(name="work", bufs=2) as work,
+        tc.psum_pool(name="hidden_psum", bufs=4) as hidden_psum,
+        tc.psum_pool(name="logit_psum", bufs=1) as logit_psum,
+    ):
+        offsets = held.tile([P, ENTRIES // 16], U16, name="offsets")
+        nc.sync.dma_start(offsets[:], offs)
+        words = held.tile([P, WORDS], BF16, name="words")
+        nc.scalar.dma_start(words[:], table)
+        project = held.tile([P, HIDDEN_BLOCKS * P], BF16, name="project")
+        nc.sync.dma_start(project[:], w1)
+        score_rows = held.tile([P, ENTRIES], F32, name="score_rows")
+        nc.scalar.dma_start(score_rows[:], scores[0, :].partition_broadcast(P))
+        classify = held.tile([P, HIDDEN_BLOCKS, LABELS], BF16, name="classify")
+        nc.sync.dma_start(classify[:], wout.rearrange("(k p) r -> p k r", p=P))
+        hidden_bias = []
+        for k in range(HIDDEN_BLOCKS):
+            column = held.tile([P, 1], F32, name=f"hidden_bias{k}")
+            nc.gpsimd.dma_start(column[:], b1[k * P : (k + 1) * P, :])
+            hidden_bias.append(column)
+        label_bias = held.tile([1, LABELS], F32, name="label_bias")
+        nc.gpsimd.dma_start(label_bias[:], bout.rearrange("r o -> o r"))
+        ones = held.tile([1, SENTENCES], F32, name="ones")
+        nc.vector.memset(ones[:], 1.0)
+
+        banks = []
+        for k in range(HIDDEN_BLOCKS):
+            for half in range(ENTRIES // BANK):
+                bank = hidden_psum.tile([P, BANK], F32, name="bank")
+                for piece in range(BANK // PIECE):
+                    first = half * BANK + piece * PIECE
+                    nc.tensor.matmul(
+                        bank[:, piece * PIECE : (piece + 1) * PIECE],
+                        project[:, k * P : (k + 1) * P],
+                        words[:].indirect(offsets[:, first // 16 : (first + PIECE) // 16]),
+                        start=True,
+                        stop=True,
+                    )
+                banks.append(bank)
+
+        logits = logit_psum.tile([SENTENCES, LABELS], F32, name="logits")
+        for k in range(HIDDEN_BLOCKS):
+            sums = work.tile([P, SENTENCES], F32, name="sums")
+            for half in range(ENTRIES // BANK):
+                bank = banks[k * (ENTRIES // BANK) + half]
+                weighted = work.tile([P, BANK], F32, name="weighted")
+                nc.vector.tensor_tensor(
+                    weighted[:], bank[:], score_rows[:, half * BANK : (half + 1) * BANK], ALU.mult
+                )
+                per_bank = BANK // PER_SENTENCE
+                nc.vector.tensor_reduce(
+                    sums[:, half * per_bank : (half + 1) * per_bank],
+                    weighted[:].rearrange("p (i t) -> p i t", t=PER_SENTENCE),
+                    axis=mybir.AxisListType.X,
+                    op=ALU.add,
+                )
+            pooled = work.tile([P, SENTENCES], BF16, name="pooled")
+            nc.scalar.activation(
+                pooled[:], sums[:], ACT.Identity, bias=hidden_bias[k][:], scale=1.0 / PER_SENTENCE
+            )
+            if k == 0:
+                nc.tensor.matmul(logits[:], ones[:], label_bias[:], start=True, stop=False)
+            nc.tensor.matmul(
+                logits[:], pooled[:], classify[:, k, :], start=False, stop=(k == HIDDEN_BLOCKS - 1)
+            )
+
+        minus_top = work.tile([SENTENCES, 1], F32, name="minus_top")
+        nc.vector.tensor_reduce(
+            minus_top[:], logits[:], axis=mybir.AxisListType.X, op=ALU.max, negate=True
+        )
+        powers = work.tile([SENTENCES, LABELS], F32, name="powers")
+        total = work.tile([SENTENCES, 1], F32, name="total")
+        nc.scalar.activation(powers[:], logits[:], ACT.Exp, bias=minus_top[:], accum_out=total[:])
+        log_total = work.tile([SENTENCES, 1], F32, name="log_total")
+        nc.scalar.activation(log_total[:], total[:], ACT.Ln)
+        result = work.tile([SENTENCES, LABELS], F32, name="result")
+        nc.vector.tensor_scalar(
+            result[:], logits[:], minus_top[:], log_total[:], op0=ALU.add, op1=ALU.subtract
+        )
+        nc.sync.dma_start(out, result[:])

@@ -44,6 +44,9 @@ def tile_dnn_kernel(tc, table, w1, scores, b1, wout, bout, offs, out):
         nc.gpsimd.dma_start(label_bias[:], bout.rearrange("r o -> o r"))
         ones = held.tile([1, SENTENCES], F32, name="ones")
         nc.vector.memset(ones[:], 1.0)
+        scratch = held.tile([P, 1], F32, name="scratch")
+        nc.vector.memset(scratch[:], 1.0)
+        nc.scalar.activation(scratch[:], scratch[:], ACT.Ln)
 
         banks = []
         for k in range(HIDDEN_BLOCKS):

@@ -31,22 +31,22 @@ def tile_dnn_kernel(tc, table, w1, scores, b1, wout, bout, offs, out):
         nc.scalar.dma_start(words[:], table)
         project = held.tile([P, HIDDEN_BLOCKS * P], BF16, name="project")
         nc.sync.dma_start(project[:], w1)
-        score_rows = held.tile([P, ENTRIES], F32, name="score_rows")
-        nc.scalar.dma_start(score_rows[:], scores[0, :].partition_broadcast(P))
-        classify = held.tile([P, HIDDEN_BLOCKS, LABELS], BF16, name="classify")
-        nc.sync.dma_start(classify[:], wout.rearrange("(k p) r -> p k r", p=P))
+        score_rows = []
+        for half, queue in enumerate((nc.scalar, nc.sync)):
+            rows = held.tile([P, BANK], F32, name=f"score_rows{half}")
+            queue.dma_start(rows[:], scores[0, half * BANK : (half + 1) * BANK].partition_broadcast(P))
+            score_rows.append(rows)
         hidden_bias = []
-        for k in range(HIDDEN_BLOCKS):
+        for k, queue in enumerate((nc.scalar, nc.sync)):
             column = held.tile([P, 1], F32, name=f"hidden_bias{k}")
-            nc.gpsimd.dma_start(column[:], b1[k * P : (k + 1) * P, :])
+            queue.dma_start(column[:], b1[k * P : (k + 1) * P, :])
             hidden_bias.append(column)
+        classify = held.tile([P, HIDDEN_BLOCKS, LABELS], BF16, name="classify")
+        nc.scalar.dma_start(classify[:], wout.rearrange("(k p) r -> p k r", p=P))
         label_bias = held.tile([1, LABELS], F32, name="label_bias")
-        nc.gpsimd.dma_start(label_bias[:], bout.rearrange("r o -> o r"))
+        nc.sync.dma_start(label_bias[:], bout.rearrange("r o -> o r"))
         ones = held.tile([1, SENTENCES], F32, name="ones")
         nc.vector.memset(ones[:], 1.0)
-        scratch = held.tile([P, 1], F32, name="scratch")
-        nc.vector.memset(scratch[:], 1.0)
-        nc.scalar.activation(scratch[:], scratch[:], ACT.Ln)
 
         banks = []
         for k in range(HIDDEN_BLOCKS):
@@ -70,7 +70,7 @@ def tile_dnn_kernel(tc, table, w1, scores, b1, wout, bout, offs, out):
                 bank = banks[k * (ENTRIES // BANK) + half]
                 weighted = work.tile([P, BANK], F32, name="weighted")
                 nc.vector.tensor_tensor(
-                    weighted[:], bank[:], score_rows[:, half * BANK : (half + 1) * BANK], ALU.mult
+                    weighted[:], bank[:], score_rows[half][:], ALU.mult
                 )
                 per_bank = BANK // PER_SENTENCE
                 nc.vector.tensor_reduce(

@@ -13,6 +13,7 @@ PER_SENTENCE = 8
 ENTRIES = SENTENCES * PER_SENTENCE
 PIECE = 256
 BANK = 512
+WARM_UP = 4
 
 FLOPS = 2 * P * HIDDEN_BLOCKS * P * ENTRIES + 2 * HIDDEN_BLOCKS * P * SENTENCES * LABELS
 
@@ -21,9 +22,11 @@ def tile_dnn_kernel(tc, table, w1, scores, b1, wout, bout, offs, out):
     nc = tc.nc
     with (
         tc.tile_pool(name="held", bufs=1) as held,
-        tc.tile_pool(name="work", bufs=2) as work,
+        tc.tile_pool(name="work", bufs=3) as work,
         tc.psum_pool(name="hidden_psum", bufs=4) as hidden_psum,
         tc.psum_pool(name="logit_psum", bufs=1) as logit_psum,
+        tc.psum_pool(name="bias_psum", bufs=1) as bias_psum,
+        tc.psum_pool(name="spare_psum", bufs=1) as spare_psum,
     ):
         offsets = held.tile([P, ENTRIES // 16], U16, name="offsets")
         nc.sync.dma_start(offsets[:], offs)
@@ -31,22 +34,22 @@ def tile_dnn_kernel(tc, table, w1, scores, b1, wout, bout, offs, out):
         nc.scalar.dma_start(words[:], table)
         project = held.tile([P, HIDDEN_BLOCKS * P], BF16, name="project")
         nc.sync.dma_start(project[:], w1)
-        score_rows = []
-        for half, queue in enumerate((nc.scalar, nc.sync)):
-            rows = held.tile([P, BANK], F32, name=f"score_rows{half}")
-            queue.dma_start(rows[:], scores[0, half * BANK : (half + 1) * BANK].partition_broadcast(P))
-            score_rows.append(rows)
-        hidden_bias = []
-        for k, queue in enumerate((nc.scalar, nc.sync)):
-            column = held.tile([P, 1], F32, name=f"hidden_bias{k}")
-            queue.dma_start(column[:], b1[k * P : (k + 1) * P, :])
-            hidden_bias.append(column)
+        score_rows = held.tile([P, ENTRIES], F32, name="score_rows")
+        nc.scalar.dma_start(score_rows[:], scores[0, :].partition_broadcast(P))
         classify = held.tile([P, HIDDEN_BLOCKS, LABELS], BF16, name="classify")
-        nc.scalar.dma_start(classify[:], wout.rearrange("(k p) r -> p k r", p=P))
+        nc.sync.dma_start(classify[:], wout.rearrange("(k p) r -> p k r", p=P))
+        hidden_bias_row = held.tile([1, HIDDEN_BLOCKS * P], F32, name="hidden_bias_row")
+        nc.scalar.dma_start(hidden_bias_row[:], b1.rearrange("m o -> o m"))
         label_bias = held.tile([1, LABELS], F32, name="label_bias")
         nc.sync.dma_start(label_bias[:], bout.rearrange("r o -> o r"))
         ones = held.tile([1, SENTENCES], F32, name="ones")
         nc.vector.memset(ones[:], 1.0)
+
+        zeros = held.tile([P, BANK], BF16, name="zeros")
+        nc.gpsimd.memset(zeros[:], 0.0)
+        unused = spare_psum.tile([P, BANK], F32, name="unused")
+        for turn in range(WARM_UP):
+            nc.tensor.matmul(unused[:], zeros[:, 0:P], zeros[:], start=True, stop=True)
 
         banks = []
         for k in range(HIDDEN_BLOCKS):
@@ -63,6 +66,18 @@ def tile_dnn_kernel(tc, table, w1, scores, b1, wout, bout, offs, out):
                     )
                 banks.append(bank)
 
+        turned = bias_psum.tile([P, HIDDEN_BLOCKS], F32, name="turned")
+        for k in range(HIDDEN_BLOCKS):
+            nc.tensor.matmul(
+                turned[:, k : k + 1],
+                hidden_bias_row[:, k * P : (k + 1) * P],
+                ones[:, 0:1],
+                start=True,
+                stop=True,
+            )
+        hidden_bias = held.tile([P, HIDDEN_BLOCKS], F32, name="hidden_bias")
+        nc.scalar.copy(hidden_bias[:], turned[:])
+
         logits = logit_psum.tile([SENTENCES, LABELS], F32, name="logits")
         for k in range(HIDDEN_BLOCKS):
             sums = work.tile([P, SENTENCES], F32, name="sums")
@@ -70,18 +85,28 @@ def tile_dnn_kernel(tc, table, w1, scores, b1, wout, bout, offs, out):
                 bank = banks[k * (ENTRIES // BANK) + half]
                 weighted = work.tile([P, BANK], F32, name="weighted")
                 nc.vector.tensor_tensor(
-                    weighted[:], bank[:], score_rows[half][:], ALU.mult
+                    weighted[:], bank[:], score_rows[:, half * BANK : (half + 1) * BANK], ALU.mult
                 )
+                by_sentence = weighted[:].rearrange("p (i t) -> p i t", t=PER_SENTENCE)
                 per_bank = BANK // PER_SENTENCE
+                if bank is not banks[-1]:
+                    folded = work.tile([P, per_bank, PER_SENTENCE // 2], F32, name="folded")
+                    nc.gpsimd.tensor_tensor(
+                        folded[:],
+                        by_sentence[:, :, 0 : PER_SENTENCE // 2],
+                        by_sentence[:, :, PER_SENTENCE // 2 : PER_SENTENCE],
+                        ALU.add,
+                    )
+                    by_sentence = folded[:]
                 nc.vector.tensor_reduce(
                     sums[:, half * per_bank : (half + 1) * per_bank],
-                    weighted[:].rearrange("p (i t) -> p i t", t=PER_SENTENCE),
+                    by_sentence,
                     axis=mybir.AxisListType.X,
                     op=ALU.add,
                 )
             pooled = work.tile([P, SENTENCES], BF16, name="pooled")
             nc.scalar.activation(
-                pooled[:], sums[:], ACT.Identity, bias=hidden_bias[k][:], scale=1.0 / PER_SENTENCE
+                pooled[:], sums[:], ACT.Identity, bias=hidden_bias[:, k : k + 1], scale=1.0 / PER_SENTENCE
             )
             if k == 0:
                 nc.tensor.matmul(logits[:], ones[:], label_bias[:], start=True, stop=False)

@@ -22,7 +22,7 @@ def tile_dnn_kernel(tc, table, w1, scores, b1, wout, bout, offs, out):
     nc = tc.nc
     with (
         tc.tile_pool(name="held", bufs=1) as held,
-        tc.tile_pool(name="work", bufs=3) as work,
+        tc.tile_pool(name="work", bufs=2) as work,
         tc.psum_pool(name="hidden_psum", bufs=4) as hidden_psum,
         tc.psum_pool(name="logit_psum", bufs=1) as logit_psum,
         tc.psum_pool(name="bias_psum", bufs=1) as bias_psum,
@@ -87,20 +87,10 @@ def tile_dnn_kernel(tc, table, w1, scores, b1, wout, bout, offs, out):
                 nc.vector.tensor_tensor(
                     weighted[:], bank[:], score_rows[:, half * BANK : (half + 1) * BANK], ALU.mult
                 )
-                by_sentence = weighted[:].rearrange("p (i t) -> p i t", t=PER_SENTENCE)
                 per_bank = BANK // PER_SENTENCE
-                if bank is not banks[-1]:
-                    folded = work.tile([P, per_bank, PER_SENTENCE // 2], F32, name="folded")
-                    nc.gpsimd.tensor_tensor(
-                        folded[:],
-                        by_sentence[:, :, 0 : PER_SENTENCE // 2],
-                        by_sentence[:, :, PER_SENTENCE // 2 : PER_SENTENCE],
-                        ALU.add,
-                    )
-                    by_sentence = folded[:]
                 nc.vector.tensor_reduce(
                     sums[:, half * per_bank : (half + 1) * per_bank],
-                    by_sentence,
+                    weighted[:].rearrange("p (i t) -> p i t", t=PER_SENTENCE),
                     axis=mybir.AxisListType.X,
                     op=ALU.add,
                 )

@@ -13,7 +13,6 @@ PER_SENTENCE = 8
 ENTRIES = SENTENCES * PER_SENTENCE
 PIECE = 256
 BANK = 512
-WARM_UP = 4
 
 FLOPS = 2 * P * HIDDEN_BLOCKS * P * ENTRIES + 2 * HIDDEN_BLOCKS * P * SENTENCES * LABELS
 
@@ -22,11 +21,10 @@ def tile_dnn_kernel(tc, table, w1, scores, b1, wout, bout, offs, out):
     nc = tc.nc
     with (
         tc.tile_pool(name="held", bufs=1) as held,
-        tc.tile_pool(name="work", bufs=2) as work,
+        tc.tile_pool(name="work", bufs=3) as work,
         tc.psum_pool(name="hidden_psum", bufs=4) as hidden_psum,
         tc.psum_pool(name="logit_psum", bufs=1) as logit_psum,
         tc.psum_pool(name="bias_psum", bufs=1) as bias_psum,
-        tc.psum_pool(name="spare_psum", bufs=1) as spare_psum,
     ):
         offsets = held.tile([P, ENTRIES // 16], U16, name="offsets")
         nc.sync.dma_start(offsets[:], offs)
@@ -44,12 +42,6 @@ def tile_dnn_kernel(tc, table, w1, scores, b1, wout, bout, offs, out):
         nc.sync.dma_start(label_bias[:], bout.rearrange("r o -> o r"))
         ones = held.tile([1, SENTENCES], F32, name="ones")
         nc.vector.memset(ones[:], 1.0)
-
-        zeros = held.tile([P, BANK], BF16, name="zeros")
-        nc.gpsimd.memset(zeros[:], 0.0)
-        unused = spare_psum.tile([P, BANK], F32, name="unused")
-        for turn in range(WARM_UP):
-            nc.tensor.matmul(unused[:], zeros[:, 0:P], zeros[:], start=True, stop=True)
 
         banks = []
         for k in range(HIDDEN_BLOCKS):
@@ -87,10 +79,20 @@ def tile_dnn_kernel(tc, table, w1, scores, b1, wout, bout, offs, out):
                 nc.vector.tensor_tensor(
                     weighted[:], bank[:], score_rows[:, half * BANK : (half + 1) * BANK], ALU.mult
                 )
+                by_sentence = weighted[:].rearrange("p (i t) -> p i t", t=PER_SENTENCE)
                 per_bank = BANK // PER_SENTENCE
+                if bank is not banks[-1]:
+                    folded = work.tile([P, per_bank, PER_SENTENCE // 2], F32, name="folded")
+                    nc.gpsimd.tensor_tensor(
+                        folded[:],
+                        by_sentence[:, :, 0 : PER_SENTENCE // 2],
+                        by_sentence[:, :, PER_SENTENCE // 2 : PER_SENTENCE],
+                        ALU.add,
+                    )
+                    by_sentence = folded[:]
                 nc.vector.tensor_reduce(
                     sums[:, half * per_bank : (half + 1) * per_bank],
-                    weighted[:].rearrange("p (i t) -> p i t", t=PER_SENTENCE),
+                    by_sentence,
                     axis=mybir.AxisListType.X,
                     op=ALU.add,
                 )

@@ -1,6 +1,6 @@
 import concourse.mybir as mybir
 
-BF16, F32, U16 = mybir.dt.bfloat16, mybir.dt.float32, mybir.dt.uint16
+BF16, F32, U16, U32 = mybir.dt.bfloat16, mybir.dt.float32, mybir.dt.uint16, mybir.dt.uint32
 ALU = mybir.AluOpType
 ACT = mybir.ActivationFunctionType
 
@@ -13,6 +13,9 @@ PER_SENTENCE = 8
 ENTRIES = SENTENCES * PER_SENTENCE
 PIECE = 256
 BANK = 512
+LN2 = 0.6931471805599453
+MANTISSA = 2.0**23
+HUMP = 0.0860713320559342
 
 FLOPS = 2 * P * HIDDEN_BLOCKS * P * ENTRIES + 2 * HIDDEN_BLOCKS * P * SENTENCES * LABELS
 
@@ -113,8 +116,26 @@ def tile_dnn_kernel(tc, table, w1, scores, b1, wout, bout, offs, out):
         powers = work.tile([SENTENCES, LABELS], F32, name="powers")
         total = work.tile([SENTENCES, 1], F32, name="total")
         nc.scalar.activation(powers[:], logits[:], ACT.Exp, bias=minus_top[:], accum_out=total[:])
+        minus_guess = work.tile([SENTENCES, 1], F32, name="minus_guess")
+        nc.scalar.activation(
+            minus_guess[:],
+            total[:].bitcast(U32),
+            ACT.Copy,
+            bias=LN2 * (127.0 - HUMP / 2.0),
+            scale=-LN2 / MANTISSA,
+        )
+        shrink = work.tile([SENTENCES, 1], F32, name="shrink")
+        nc.scalar.activation(shrink[:], minus_guess[:], ACT.Exp)
+        excess = work.tile([SENTENCES, 1], F32, name="excess")
+        nc.vector.tensor_scalar(excess[:], shrink[:], total[:], -1.0, op0=ALU.mult, op1=ALU.add)
+        inner = work.tile([SENTENCES, 1], F32, name="inner")
+        nc.vector.tensor_scalar(inner[:], excess[:], 1.0 / 3.0, -0.5, op0=ALU.mult, op1=ALU.add)
+        outer = work.tile([SENTENCES, 1], F32, name="outer")
+        nc.vector.tensor_scalar(outer[:], inner[:], excess[:], 1.0, op0=ALU.mult, op1=ALU.add)
         log_total = work.tile([SENTENCES, 1], F32, name="log_total")
-        nc.scalar.activation(log_total[:], total[:], ACT.Ln)
+        nc.vector.tensor_scalar(
+            log_total[:], outer[:], excess[:], minus_guess[:], op0=ALU.mult, op1=ALU.subtract
+        )
         result = work.tile([SENTENCES, LABELS], F32, name="result")
         nc.vector.tensor_scalar(
             result[:], logits[:], minus_top[:], log_total[:], op0=ALU.add, op1=ALU.subtract

@@ -13,9 +13,13 @@ PER_SENTENCE = 8
 ENTRIES = SENTENCES * PER_SENTENCE
 PIECE = 256
 BANK = 512
+
 LN2 = 0.6931471805599453
+ROOT2 = 1.4142135623730951
 MANTISSA = 2.0**23
 HUMP = 0.0860713320559342
+SPAN = LN2 * HUMP / 2.0
+SLOPE = 1.0 + SPAN * SPAN / 4.0
 
 FLOPS = 2 * P * HIDDEN_BLOCKS * P * ENTRIES + 2 * HIDDEN_BLOCKS * P * SENTENCES * LABELS
 
@@ -116,28 +120,29 @@ def tile_dnn_kernel(tc, table, w1, scores, b1, wout, bout, offs, out):
         powers = work.tile([SENTENCES, LABELS], F32, name="powers")
         total = work.tile([SENTENCES, 1], F32, name="total")
         nc.scalar.activation(powers[:], logits[:], ACT.Exp, bias=minus_top[:], accum_out=total[:])
+        bits_scale = -LN2 / MANTISSA
+        bits_bias = LN2 * (127.0 - HUMP / 2.0) - LN2 / 2.0
+        shrink = work.tile([SENTENCES, 1], F32, name="shrink")
+        nc.scalar.activation(
+            shrink[:], total[:].bitcast(U32), ACT.Exp, bias=bits_bias, scale=bits_scale
+        )
         minus_guess = work.tile([SENTENCES, 1], F32, name="minus_guess")
         nc.scalar.activation(
-            minus_guess[:],
-            total[:].bitcast(U32),
-            ACT.Copy,
-            bias=LN2 * (127.0 - HUMP / 2.0),
-            scale=-LN2 / MANTISSA,
+            minus_guess[:], total[:].bitcast(U32), ACT.Copy, bias=bits_bias, scale=bits_scale
         )
-        shrink = work.tile([SENTENCES, 1], F32, name="shrink")
-        nc.scalar.activation(shrink[:], minus_guess[:], ACT.Exp)
-        excess = work.tile([SENTENCES, 1], F32, name="excess")
-        nc.vector.tensor_scalar(excess[:], shrink[:], total[:], -1.0, op0=ALU.mult, op1=ALU.add)
-        inner = work.tile([SENTENCES, 1], F32, name="inner")
-        nc.vector.tensor_scalar(inner[:], excess[:], 1.0 / 3.0, -0.5, op0=ALU.mult, op1=ALU.add)
-        outer = work.tile([SENTENCES, 1], F32, name="outer")
-        nc.vector.tensor_scalar(outer[:], inner[:], excess[:], 1.0, op0=ALU.mult, op1=ALU.add)
-        log_total = work.tile([SENTENCES, 1], F32, name="log_total")
+        square = work.tile([SENTENCES, 1], F32, name="square")
+        nc.scalar.activation(
+            square[:], shrink[:], ACT.Square, bias=-(1.0 + SLOPE) / ROOT2, scale=total[:]
+        )
+        shift = work.tile([SENTENCES, 1], F32, name="shift")
         nc.vector.tensor_scalar(
-            log_total[:], outer[:], excess[:], minus_guess[:], op0=ALU.mult, op1=ALU.subtract
+            shift[:],
+            minus_guess[:],
+            minus_top[:],
+            LN2 / 2.0 - SLOPE * SLOPE / 2.0,
+            op0=ALU.add,
+            op1=ALU.add,
         )
         result = work.tile([SENTENCES, LABELS], F32, name="result")
-        nc.vector.tensor_scalar(
-            result[:], logits[:], minus_top[:], log_total[:], op0=ALU.add, op1=ALU.subtract
-        )
+        nc.vector.tensor_scalar(result[:], logits[:], shift[:], square[:], op0=ALU.add, op1=ALU.add)
         nc.sync.dma_start(out, result[:])

@@ -13,6 +13,8 @@ PER_SENTENCE = 8
 ENTRIES = SENTENCES * PER_SENTENCE
 PIECE = 256
 BANK = 512
+PER_BANK = BANK // PER_SENTENCE
+LINE = 4
 
 LN2 = 0.6931471805599453
 ROOT2 = 1.4142135623730951
@@ -31,7 +33,6 @@ def tile_dnn_kernel(tc, table, w1, scores, b1, wout, bout, offs, out):
         tc.tile_pool(name="work", bufs=3) as work,
         tc.psum_pool(name="hidden_psum", bufs=4) as hidden_psum,
         tc.psum_pool(name="logit_psum", bufs=1) as logit_psum,
-        tc.psum_pool(name="bias_psum", bufs=1) as bias_psum,
     ):
         offsets = held.tile([P, ENTRIES // 16], U16, name="offsets")
         nc.sync.dma_start(offsets[:], offs)
@@ -43,8 +44,8 @@ def tile_dnn_kernel(tc, table, w1, scores, b1, wout, bout, offs, out):
         nc.scalar.dma_start(score_rows[:], scores[0, :].partition_broadcast(P))
         classify = held.tile([P, HIDDEN_BLOCKS, LABELS], BF16, name="classify")
         nc.sync.dma_start(classify[:], wout.rearrange("(k p) r -> p k r", p=P))
-        hidden_bias_row = held.tile([1, HIDDEN_BLOCKS * P], F32, name="hidden_bias_row")
-        nc.scalar.dma_start(hidden_bias_row[:], b1.rearrange("m o -> o m"))
+        hidden_bias = held.tile([P, HIDDEN_BLOCKS], F32, name="hidden_bias")
+        nc.scalar.dma_start(hidden_bias[:], b1.rearrange("(k p) o -> p (k o)", p=P))
         label_bias = held.tile([1, LABELS], F32, name="label_bias")
         nc.sync.dma_start(label_bias[:], bout.rearrange("r o -> o r"))
         ones = held.tile([1, SENTENCES], F32, name="ones")
@@ -65,52 +66,57 @@ def tile_dnn_kernel(tc, table, w1, scores, b1, wout, bout, offs, out):
                     )
                 banks.append(bank)
 
-        turned = bias_psum.tile([P, HIDDEN_BLOCKS], F32, name="turned")
-        for k in range(HIDDEN_BLOCKS):
-            nc.tensor.matmul(
-                turned[:, k : k + 1],
-                hidden_bias_row[:, k * P : (k + 1) * P],
-                ones[:, 0:1],
-                start=True,
-                stop=True,
+        classify_eighth = held.tile([P, HIDDEN_BLOCKS, LABELS], BF16, name="classify_eighth")
+        nc.scalar.mul(classify_eighth[:], classify[:], 1.0 / PER_SENTENCE)
+        eights = held.tile([P, PER_BANK, 1], F32, name="eights")
+        nc.vector.memset(eights[:], float(PER_SENTENCE))
+        terms = []
+        for b in range(len(banks)):
+            count = PER_SENTENCE if b == len(banks) - 1 else PER_SENTENCE // 2
+            of_bank = held.tile([P, PER_BANK, count + LINE], F32, name="terms%d" % b)
+            k = b // (ENTRIES // BANK)
+            nc.scalar.activation(
+                of_bank[:, :, count : count + 1], eights[:], ACT.Identity, scale=hidden_bias[:, k : k + 1]
             )
-        hidden_bias = held.tile([P, HIDDEN_BLOCKS], F32, name="hidden_bias")
-        nc.scalar.copy(hidden_bias[:], turned[:])
+            terms.append((of_bank, count))
 
         logits = logit_psum.tile([SENTENCES, LABELS], F32, name="logits")
         for k in range(HIDDEN_BLOCKS):
-            sums = work.tile([P, SENTENCES], F32, name="sums")
+            pooled = work.tile([P, SENTENCES], BF16, name="pooled")
             for half in range(ENTRIES // BANK):
-                bank = banks[k * (ENTRIES // BANK) + half]
-                weighted = work.tile([P, BANK], F32, name="weighted")
-                nc.vector.tensor_tensor(
-                    weighted[:], bank[:], score_rows[:, half * BANK : (half + 1) * BANK], ALU.mult
+                b = k * (ENTRIES // BANK) + half
+                of_bank, count = terms[b]
+                by_sentence = "p (i t) -> p i t"
+                hidden = banks[b][:].rearrange(by_sentence, t=PER_SENTENCE)
+                weights = score_rows[:, half * BANK : (half + 1) * BANK].rearrange(
+                    by_sentence, t=PER_SENTENCE
                 )
-                by_sentence = weighted[:].rearrange("p (i t) -> p i t", t=PER_SENTENCE)
-                per_bank = BANK // PER_SENTENCE
-                if bank is not banks[-1]:
-                    folded = work.tile([P, per_bank, PER_SENTENCE // 2], F32, name="folded")
+                if count == PER_SENTENCE:
+                    nc.vector.tensor_tensor(of_bank[:, :, 0:count], hidden, weights, ALU.mult)
+                else:
+                    weighted = work.tile([P, PER_BANK, PER_SENTENCE], F32, name="weighted")
+                    nc.vector.tensor_tensor(weighted[:], hidden, weights, ALU.mult)
                     nc.gpsimd.tensor_tensor(
-                        folded[:],
-                        by_sentence[:, :, 0 : PER_SENTENCE // 2],
-                        by_sentence[:, :, PER_SENTENCE // 2 : PER_SENTENCE],
+                        of_bank[:, :, 0:count],
+                        weighted[:, :, 0:count],
+                        weighted[:, :, count:PER_SENTENCE],
                         ALU.add,
                     )
-                    by_sentence = folded[:]
-                nc.vector.tensor_reduce(
-                    sums[:, half * per_bank : (half + 1) * per_bank],
-                    by_sentence,
-                    axis=mybir.AxisListType.X,
-                    op=ALU.add,
-                )
-            pooled = work.tile([P, SENTENCES], BF16, name="pooled")
-            nc.scalar.activation(
-                pooled[:], sums[:], ACT.Identity, bias=hidden_bias[:, k : k + 1], scale=1.0 / PER_SENTENCE
-            )
+                with nc.allow_low_precision(reason="the sum is made in float32; x is rounded once"):
+                    nc.vector.tensor_reduce(
+                        pooled[:, half * PER_BANK : (half + 1) * PER_BANK],
+                        of_bank[:, :, 0 : count + 1],
+                        axis=mybir.AxisListType.X,
+                        op=ALU.add,
+                    )
             if k == 0:
                 nc.tensor.matmul(logits[:], ones[:], label_bias[:], start=True, stop=False)
             nc.tensor.matmul(
-                logits[:], pooled[:], classify[:, k, :], start=False, stop=(k == HIDDEN_BLOCKS - 1)
+                logits[:],
+                pooled[:],
+                classify_eighth[:, k, :],
+                start=False,
+                stop=(k == HIDDEN_BLOCKS - 1),
             )
 
         minus_top = work.tile([SENTENCES, 1], F32, name="minus_top")

@@ -81,13 +81,13 @@ def tile_dnn_kernel(tc, table, w1, scores, b1, wout, bout, offs, out):
             terms.append((of_bank, count))
 
         logits = logit_psum.tile([SENTENCES, LABELS], F32, name="logits")
+        by_sentence = "p (i t) -> p i t"
         for k in range(HIDDEN_BLOCKS):
             pooled = work.tile([P, SENTENCES], BF16, name="pooled")
-            for half in range(ENTRIES // BANK):
-                b = k * (ENTRIES // BANK) + half
-                of_bank, count = terms[b]
-                by_sentence = "p (i t) -> p i t"
-                hidden = banks[b][:].rearrange(by_sentence, t=PER_SENTENCE)
+            halves = list(range(ENTRIES // BANK))
+            for half in halves:
+                of_bank, count = terms[k * (ENTRIES // BANK) + half]
+                hidden = banks[k * (ENTRIES // BANK) + half][:].rearrange(by_sentence, t=PER_SENTENCE)
                 weights = score_rows[:, half * BANK : (half + 1) * BANK].rearrange(
                     by_sentence, t=PER_SENTENCE
                 )
@@ -102,6 +102,10 @@ def tile_dnn_kernel(tc, table, w1, scores, b1, wout, bout, offs, out):
                         weighted[:, :, count:PER_SENTENCE],
                         ALU.add,
                     )
+            if k == HIDDEN_BLOCKS - 1:
+                halves = list(reversed(halves))
+            for half in halves:
+                of_bank, count = terms[k * (ENTRIES // BANK) + half]
                 with nc.allow_low_precision(reason="the sum is made in float32; x is rounded once"):
                     nc.vector.tensor_reduce(
                         pooled[:, half * PER_BANK : (half + 1) * PER_BANK],

@@ -68,16 +68,18 @@ def tile_dnn_kernel(tc, table, w1, scores, b1, wout, bout, offs, out):
 
         classify_eighth = held.tile([P, HIDDEN_BLOCKS, LABELS], BF16, name="classify_eighth")
         nc.scalar.mul(classify_eighth[:], classify[:], 1.0 / PER_SENTENCE)
-        eights = held.tile([P, PER_BANK, 1], F32, name="eights")
-        nc.vector.memset(eights[:], float(PER_SENTENCE))
+        bias_eightfold = held.tile([P, HIDDEN_BLOCKS], F32, name="bias_eightfold")
+        nc.scalar.mul(bias_eightfold[:], hidden_bias[:], float(PER_SENTENCE))
+        last = HIDDEN_BLOCKS - 1
         terms = []
         for b in range(len(banks)):
             count = PER_SENTENCE if b == len(banks) - 1 else PER_SENTENCE // 2
             of_bank = held.tile([P, PER_BANK, count + LINE], F32, name="terms%d" % b)
-            k = b // (ENTRIES // BANK)
-            nc.scalar.activation(
-                of_bank[:, :, count : count + 1], eights[:], ACT.Identity, scale=hidden_bias[:, k : k + 1]
-            )
+            if b // (ENTRIES // BANK) == last:
+                nc.scalar.copy(
+                    of_bank[:, :, count : count + 1],
+                    bias_eightfold[:, last : last + 1].unsqueeze(2).to_broadcast([P, PER_BANK, 1]),
+                )
             terms.append((of_bank, count))
 
         logits = logit_psum.tile([SENTENCES, LABELS], F32, name="logits")
@@ -102,25 +104,33 @@ def tile_dnn_kernel(tc, table, w1, scores, b1, wout, bout, offs, out):
                         weighted[:, :, count:PER_SENTENCE],
                         ALU.add,
                     )
-            if k == HIDDEN_BLOCKS - 1:
-                halves = list(reversed(halves))
-            for half in halves:
-                of_bank, count = terms[k * (ENTRIES // BANK) + half]
-                with nc.allow_low_precision(reason="the sum is made in float32; x is rounded once"):
+            if k == last:
+                for half in reversed(halves):
+                    of_bank, count = terms[k * (ENTRIES // BANK) + half]
+                    with nc.allow_low_precision(reason="the sum is made in float32; x is rounded once"):
+                        nc.vector.tensor_reduce(
+                            pooled[:, half * PER_BANK : (half + 1) * PER_BANK],
+                            of_bank[:, :, 0 : count + 1],
+                            axis=mybir.AxisListType.X,
+                            op=ALU.add,
+                        )
+            else:
+                sums = work.tile([P, SENTENCES], F32, name="sums")
+                for half in halves:
+                    of_bank, count = terms[k * (ENTRIES // BANK) + half]
                     nc.vector.tensor_reduce(
-                        pooled[:, half * PER_BANK : (half + 1) * PER_BANK],
-                        of_bank[:, :, 0 : count + 1],
+                        sums[:, half * PER_BANK : (half + 1) * PER_BANK],
+                        of_bank[:, :, 0:count],
                         axis=mybir.AxisListType.X,
                         op=ALU.add,
                     )
+                nc.scalar.activation(
+                    pooled[:], sums[:], ACT.Identity, bias=bias_eightfold[:, k : k + 1]
+                )
             if k == 0:
                 nc.tensor.matmul(logits[:], ones[:], label_bias[:], start=True, stop=False)
             nc.tensor.matmul(
-                logits[:],
-                pooled[:],
-                classify_eighth[:, k, :],
-                start=False,
-                stop=(k == HIDDEN_BLOCKS - 1),
+                logits[:], pooled[:], classify_eighth[:, k, :], start=False, stop=(k == last)
             )
 
         minus_top = work.tile([SENTENCES, 1], F32, name="minus_top")

@@ -140,6 +140,8 @@ def tile_dnn_kernel(tc, table, w1, scores, b1, wout, bout, offs, out):
         powers = work.tile([SENTENCES, LABELS], F32, name="powers")
         total = work.tile([SENTENCES, 1], F32, name="total")
         nc.scalar.activation(powers[:], logits[:], ACT.Exp, bias=minus_top[:], accum_out=total[:])
+        shifted = work.tile([SENTENCES, LABELS], F32, name="shifted")
+        nc.vector.tensor_scalar_add(shifted[:], logits[:], minus_top[:])
         bits_scale = -LN2 / MANTISSA
         bits_bias = LN2 * (127.0 - HUMP / 2.0) - LN2 / 2.0
         shrink = work.tile([SENTENCES, 1], F32, name="shrink")
@@ -148,21 +150,18 @@ def tile_dnn_kernel(tc, table, w1, scores, b1, wout, bout, offs, out):
         )
         minus_guess = work.tile([SENTENCES, 1], F32, name="minus_guess")
         nc.scalar.activation(
-            minus_guess[:], total[:].bitcast(U32), ACT.Copy, bias=bits_bias, scale=bits_scale
+            minus_guess[:],
+            total[:].bitcast(U32),
+            ACT.Copy,
+            bias=bits_bias + LN2 / 2.0 - SLOPE * SLOPE / 2.0,
+            scale=bits_scale,
         )
         square = work.tile([SENTENCES, 1], F32, name="square")
         nc.scalar.activation(
             square[:], shrink[:], ACT.Square, bias=-(1.0 + SLOPE) / ROOT2, scale=total[:]
         )
-        shift = work.tile([SENTENCES, 1], F32, name="shift")
-        nc.vector.tensor_scalar(
-            shift[:],
-            minus_guess[:],
-            minus_top[:],
-            LN2 / 2.0 - SLOPE * SLOPE / 2.0,
-            op0=ALU.add,
-            op1=ALU.add,
-        )
         result = work.tile([SENTENCES, LABELS], F32, name="result")
-        nc.vector.tensor_scalar(result[:], logits[:], shift[:], square[:], op0=ALU.add, op1=ALU.add)
+        nc.vector.tensor_scalar(
+            result[:], shifted[:], minus_guess[:], square[:], op0=ALU.add, op1=ALU.add
+        )
         nc.sync.dma_start(out, result[:])

@@ -42,12 +42,12 @@ def tile_dnn_kernel(tc, table, w1, scores, b1, wout, bout, offs, out):
         nc.sync.dma_start(project[:], w1)
         score_rows = held.tile([P, ENTRIES], F32, name="score_rows")
         nc.scalar.dma_start(score_rows[:], scores[0, :].partition_broadcast(P))
-        classify = held.tile([P, HIDDEN_BLOCKS, LABELS], BF16, name="classify")
-        nc.sync.dma_start(classify[:], wout.rearrange("(k p) r -> p k r", p=P))
         hidden_bias = held.tile([P, HIDDEN_BLOCKS], F32, name="hidden_bias")
         nc.scalar.dma_start(hidden_bias[:], b1.rearrange("(k p) o -> p (k o)", p=P))
+        classify = held.tile([P, HIDDEN_BLOCKS, LABELS], BF16, name="classify")
+        nc.scalar.dma_start(classify[:], wout.rearrange("(k p) r -> p k r", p=P))
         label_bias = held.tile([1, LABELS], F32, name="label_bias")
-        nc.sync.dma_start(label_bias[:], bout.rearrange("r o -> o r"))
+        nc.scalar.dma_start(label_bias[:], bout.rearrange("r o -> o r"))
         ones = held.tile([1, SENTENCES], F32, name="ones")
         nc.vector.memset(ones[:], 1.0)
 

@@ -14,7 +14,6 @@ ENTRIES = SENTENCES * PER_SENTENCE
 PIECE = 256
 BANK = 512
 PER_BANK = BANK // PER_SENTENCE
-LINE = 4
 
 LN2 = 0.6931471805599453
 ROOT2 = 1.4142135623730951
@@ -30,7 +29,7 @@ def tile_dnn_kernel(tc, table, w1, scores, b1, wout, bout, offs, out):
     nc = tc.nc
     with (
         tc.tile_pool(name="held", bufs=1) as held,
-        tc.tile_pool(name="work", bufs=3) as work,
+        tc.tile_pool(name="work", bufs=4) as work,
         tc.psum_pool(name="hidden_psum", bufs=4) as hidden_psum,
         tc.psum_pool(name="logit_psum", bufs=1) as logit_psum,
     ):
@@ -68,67 +67,51 @@ def tile_dnn_kernel(tc, table, w1, scores, b1, wout, bout, offs, out):
 
         classify_eighth = held.tile([P, HIDDEN_BLOCKS, LABELS], BF16, name="classify_eighth")
         nc.scalar.mul(classify_eighth[:], classify[:], 1.0 / PER_SENTENCE)
-        bias_eightfold = held.tile([P, HIDDEN_BLOCKS], F32, name="bias_eightfold")
-        nc.scalar.mul(bias_eightfold[:], hidden_bias[:], float(PER_SENTENCE))
-        last = HIDDEN_BLOCKS - 1
-        terms = []
-        for b in range(len(banks)):
-            count = PER_SENTENCE if b == len(banks) - 1 else PER_SENTENCE // 2
-            of_bank = held.tile([P, PER_BANK, count + LINE], F32, name="terms%d" % b)
-            if b // (ENTRIES // BANK) == last:
-                nc.scalar.copy(
-                    of_bank[:, :, count : count + 1],
-                    bias_eightfold[:, last : last + 1].unsqueeze(2).to_broadcast([P, PER_BANK, 1]),
-                )
-            terms.append((of_bank, count))
+        classify_float = held.tile([P, HIDDEN_BLOCKS, LABELS], F32, name="classify_float")
+        nc.scalar.copy(classify_float[:], classify[:])
+        bias_columns = held.tile([P, HIDDEN_BLOCKS, SENTENCES], F32, name="bias_columns")
+        nc.scalar.copy(
+            bias_columns[:],
+            hidden_bias[:].unsqueeze(2).to_broadcast([P, HIDDEN_BLOCKS, SENTENCES]),
+        )
 
         logits = logit_psum.tile([SENTENCES, LABELS], F32, name="logits")
+        nc.tensor.matmul(logits[:], ones[:], label_bias[:], start=True, stop=False)
+        for k in range(HIDDEN_BLOCKS):
+            nc.tensor.matmul(
+                logits[:], bias_columns[:, k, :], classify_float[:, k, :], start=False, stop=False
+            )
+
+        last = HIDDEN_BLOCKS - 1
         by_sentence = "p (i t) -> p i t"
         for k in range(HIDDEN_BLOCKS):
             pooled = work.tile([P, SENTENCES], BF16, name="pooled")
             halves = list(range(ENTRIES // BANK))
+            terms = []
             for half in halves:
-                of_bank, count = terms[k * (ENTRIES // BANK) + half]
                 hidden = banks[k * (ENTRIES // BANK) + half][:].rearrange(by_sentence, t=PER_SENTENCE)
                 weights = score_rows[:, half * BANK : (half + 1) * BANK].rearrange(
                     by_sentence, t=PER_SENTENCE
                 )
-                if count == PER_SENTENCE:
-                    nc.vector.tensor_tensor(of_bank[:, :, 0:count], hidden, weights, ALU.mult)
+                weighted = work.tile([P, PER_BANK, PER_SENTENCE], F32, name="weighted")
+                nc.vector.tensor_tensor(weighted[:], hidden, weights, ALU.mult)
+                if k == last and half == halves[-1]:
+                    terms.append(weighted)
                 else:
-                    weighted = work.tile([P, PER_BANK, PER_SENTENCE], F32, name="weighted")
-                    nc.vector.tensor_tensor(weighted[:], hidden, weights, ALU.mult)
+                    count = PER_SENTENCE // 2
+                    folded = work.tile([P, PER_BANK, count], F32, name="folded")
                     nc.gpsimd.tensor_tensor(
-                        of_bank[:, :, 0:count],
-                        weighted[:, :, 0:count],
-                        weighted[:, :, count:PER_SENTENCE],
-                        ALU.add,
+                        folded[:], weighted[:, :, 0:count], weighted[:, :, count:PER_SENTENCE], ALU.add
                     )
-            if k == last:
-                for half in reversed(halves):
-                    of_bank, count = terms[k * (ENTRIES // BANK) + half]
-                    with nc.allow_low_precision(reason="the sum is made in float32; x is rounded once"):
-                        nc.vector.tensor_reduce(
-                            pooled[:, half * PER_BANK : (half + 1) * PER_BANK],
-                            of_bank[:, :, 0 : count + 1],
-                            axis=mybir.AxisListType.X,
-                            op=ALU.add,
-                        )
-            else:
-                sums = work.tile([P, SENTENCES], F32, name="sums")
-                for half in halves:
-                    of_bank, count = terms[k * (ENTRIES // BANK) + half]
+                    terms.append(folded)
+            for half in reversed(halves) if k == last else halves:
+                with nc.allow_low_precision(reason="the sum is made in float32 and rounded once"):
                     nc.vector.tensor_reduce(
-                        sums[:, half * PER_BANK : (half + 1) * PER_BANK],
-                        of_bank[:, :, 0:count],
+                        pooled[:, half * PER_BANK : (half + 1) * PER_BANK],
+                        terms[half][:],
                         axis=mybir.AxisListType.X,
                         op=ALU.add,
                     )
-                nc.scalar.activation(
-                    pooled[:], sums[:], ACT.Identity, bias=bias_eightfold[:, k : k + 1]
-                )
-            if k == 0:
-                nc.tensor.matmul(logits[:], ones[:], label_bias[:], start=True, stop=False)
             nc.tensor.matmul(
                 logits[:], pooled[:], classify_eighth[:, k, :], start=False, stop=(k == last)
             )

import concourse.mybir as mybir

BF16, F32, U16, U32 = mybir.dt.bfloat16, mybir.dt.float32, mybir.dt.uint16, mybir.dt.uint32
ALU = mybir.AluOpType
ACT = mybir.ActivationFunctionType

P = 128
WORDS = 256
HIDDEN_BLOCKS = 2
LABELS = 128
SENTENCES = 128
PER_SENTENCE = 8
ENTRIES = SENTENCES * PER_SENTENCE
PIECE = 256
BANK = 512
PER_BANK = BANK // PER_SENTENCE

LN2 = 0.6931471805599453
ROOT2 = 1.4142135623730951
MANTISSA = 2.0**23
HUMP = 0.0860713320559342
SPAN = LN2 * HUMP / 2.0
SLOPE = 1.0 + SPAN * SPAN / 4.0

FLOPS = 2 * P * HIDDEN_BLOCKS * P * ENTRIES + 2 * HIDDEN_BLOCKS * P * SENTENCES * LABELS


def tile_dnn_kernel(tc, table, w1, scores, b1, wout, bout, offs, out):
    nc = tc.nc
    with (
        tc.tile_pool(name="held", bufs=1) as held,
        tc.tile_pool(name="work", bufs=4) as work,
        tc.psum_pool(name="hidden_psum", bufs=4) as hidden_psum,
        tc.psum_pool(name="logit_psum", bufs=1) as logit_psum,
    ):
        offsets = held.tile([P, ENTRIES // 16], U16, name="offsets")
        nc.sync.dma_start(offsets[:], offs)
        words = held.tile([P, WORDS], BF16, name="words")
        nc.scalar.dma_start(words[:], table)
        project = held.tile([P, HIDDEN_BLOCKS * P], BF16, name="project")
        nc.sync.dma_start(project[:], w1)
        score_rows = held.tile([P, ENTRIES], F32, name="score_rows")
        nc.scalar.dma_start(score_rows[:], scores[0, :].partition_broadcast(P))
        hidden_bias = held.tile([P, HIDDEN_BLOCKS], F32, name="hidden_bias")
        nc.scalar.dma_start(hidden_bias[:], b1.rearrange("(k p) o -> p (k o)", p=P))
        classify = held.tile([P, HIDDEN_BLOCKS, LABELS], BF16, name="classify")
        nc.scalar.dma_start(classify[:], wout.rearrange("(k p) r -> p k r", p=P))
        label_bias = held.tile([1, LABELS], F32, name="label_bias")
        nc.scalar.dma_start(label_bias[:], bout.rearrange("r o -> o r"))
        ones = held.tile([1, SENTENCES], F32, name="ones")
        nc.vector.memset(ones[:], 1.0)

        banks = []
        for k in range(HIDDEN_BLOCKS):
            for half in range(ENTRIES // BANK):
                bank = hidden_psum.tile([P, BANK], F32, name="bank")
                for piece in range(BANK // PIECE):
                    first = half * BANK + piece * PIECE
                    nc.tensor.matmul(
                        bank[:, piece * PIECE : (piece + 1) * PIECE],
                        project[:, k * P : (k + 1) * P],
                        words[:].indirect(offsets[:, first // 16 : (first + PIECE) // 16]),
                        start=True,
                        stop=True,
                    )
                banks.append(bank)

        classify_eighth = held.tile([P, HIDDEN_BLOCKS, LABELS], BF16, name="classify_eighth")
        nc.scalar.mul(classify_eighth[:], classify[:], 1.0 / PER_SENTENCE)
        classify_float = held.tile([P, HIDDEN_BLOCKS, LABELS], F32, name="classify_float")
        nc.scalar.copy(classify_float[:], classify[:])
        bias_columns = held.tile([P, HIDDEN_BLOCKS, SENTENCES], F32, name="bias_columns")
        nc.scalar.copy(
            bias_columns[:],
            hidden_bias[:].unsqueeze(2).to_broadcast([P, HIDDEN_BLOCKS, SENTENCES]),
        )

        logits = logit_psum.tile([SENTENCES, LABELS], F32, name="logits")
        nc.tensor.matmul(logits[:], ones[:], label_bias[:], start=True, stop=False)
        for k in range(HIDDEN_BLOCKS):
            nc.tensor.matmul(
                logits[:], bias_columns[:, k, :], classify_float[:, k, :], start=False, stop=False
            )

        last = HIDDEN_BLOCKS - 1
        by_sentence = "p (i t) -> p i t"
        for k in range(HIDDEN_BLOCKS):
            pooled = work.tile([P, SENTENCES], BF16, name="pooled")
            halves = list(range(ENTRIES // BANK))
            terms = []
            for half in halves:
                hidden = banks[k * (ENTRIES // BANK) + half][:].rearrange(by_sentence, t=PER_SENTENCE)
                weights = score_rows[:, half * BANK : (half + 1) * BANK].rearrange(
                    by_sentence, t=PER_SENTENCE
                )
                weighted = work.tile([P, PER_BANK, PER_SENTENCE], F32, name="weighted")
                nc.vector.tensor_tensor(weighted[:], hidden, weights, ALU.mult)
                if k == last and half == halves[-1]:
                    terms.append(weighted)
                else:
                    count = PER_SENTENCE // 2
                    folded = work.tile([P, PER_BANK, count], F32, name="folded")
                    nc.gpsimd.tensor_tensor(
                        folded[:], weighted[:, :, 0:count], weighted[:, :, count:PER_SENTENCE], ALU.add
                    )
                    terms.append(folded)
            for half in reversed(halves) if k == last else halves:
                with nc.allow_low_precision(reason="the sum is made in float32 and rounded once"):
                    nc.vector.tensor_reduce(
                        pooled[:, half * PER_BANK : (half + 1) * PER_BANK],
                        terms[half][:],
                        axis=mybir.AxisListType.X,
                        op=ALU.add,
                    )
            nc.tensor.matmul(
                logits[:], pooled[:], classify_eighth[:, k, :], start=False, stop=(k == last)
            )

        minus_top = work.tile([SENTENCES, 1], F32, name="minus_top")
        nc.vector.tensor_reduce(
            minus_top[:], logits[:], axis=mybir.AxisListType.X, op=ALU.max, negate=True
        )
        powers = work.tile([SENTENCES, LABELS], F32, name="powers")
        total = work.tile([SENTENCES, 1], F32, name="total")
        nc.scalar.activation(powers[:], logits[:], ACT.Exp, bias=minus_top[:], accum_out=total[:])
        shifted = work.tile([SENTENCES, LABELS], F32, name="shifted")
        nc.vector.tensor_scalar_add(shifted[:], logits[:], minus_top[:])
        bits_scale = -LN2 / MANTISSA
        bits_bias = LN2 * (127.0 - HUMP / 2.0) - LN2 / 2.0
        shrink = work.tile([SENTENCES, 1], F32, name="shrink")
        nc.scalar.activation(
            shrink[:], total[:].bitcast(U32), ACT.Exp, bias=bits_bias, scale=bits_scale
        )
        minus_guess = work.tile([SENTENCES, 1], F32, name="minus_guess")
        nc.scalar.activation(
            minus_guess[:],
            total[:].bitcast(U32),
            ACT.Copy,
            bias=bits_bias + LN2 / 2.0 - SLOPE * SLOPE / 2.0,
            scale=bits_scale,
        )
        square = work.tile([SENTENCES, 1], F32, name="square")
        nc.scalar.activation(
            square[:], shrink[:], ACT.Square, bias=-(1.0 + SLOPE) / ROOT2, scale=total[:]
        )
        result = work.tile([SENTENCES, LABELS], F32, name="result")
        nc.vector.tensor_scalar(
            result[:], shifted[:], minus_guess[:], square[:], op0=ALU.add, op1=ALU.add
        )
        nc.sync.dma_start(out, result[:])
